import numpy as np
import ml_dtypes


BF16 = ml_dtypes.bfloat16


def bf(x):
    return np.asarray(x, np.float32).astype(BF16)


def f64(x):
    return np.asarray(x).astype(np.float64)


E2M1 = np.array([0.0, 0.5, 1.0, 1.5, 2.0, 3.0, 4.0, 6.0, -0.0, -0.5, -1.0, -1.5, -2.0, -3.0, -4.0, -6.0])


def pack_weight(w, fmt):
    k, n = w.shape
    w = f64(bf(w)).reshape(k // 32, 32, n)
    amax = np.abs(w).max(1)
    if fmt == "e4m3":
        byte = np.frexp(amax)[1] - 1 + 127 - 7
    else:
        mant, ex = np.frexp(amax / 6.0)
        byte = np.where(mant > 0.5, ex, ex - 1) + 127
    byte = np.clip(np.where(amax > 0, byte, 1), 1, 254)
    scaled = (w * np.exp2(127.0 - byte)[:, None, :]).reshape(k, n).astype(np.float32)
    by_word = np.ascontiguousarray(scaled.reshape(k // 512, 128, 4, n).transpose(0, 1, 3, 2))
    if fmt == "e4m3":
        words = by_word.astype(ml_dtypes.float8_e4m3fn).view(np.uint8)
    else:
        c = by_word.astype(ml_dtypes.float4_e2m1fn).view(np.uint8) & 0xF
        words = c[..., 0::2] | (c[..., 1::2] << 4)
    return np.ascontiguousarray(words), np.ascontiguousarray(byte.astype(np.uint8).reshape(k // 512, 16, n))


def unpack_weight(words, scales, fmt):
    g, p, n, _ = words.shape
    if fmt == "e4m3":
        vals = np.ascontiguousarray(words).view(ml_dtypes.float8_e4m3fn).astype(np.float64)
    else:
        nib = np.empty((g, p, n, 4), np.uint8)
        nib[..., 0::2] = words & 0xF
        nib[..., 1::2] = words >> 4
        vals = E2M1[nib]
    vals = vals * np.repeat(np.exp2(scales.astype(np.float64) - 127.0), 8, axis=1)[..., None]
    return vals.transpose(0, 1, 3, 2).reshape(g * 512, n)

def pack4(w):
    words, scales = pack_weight(w, "e2m1")
    return words.reshape(words.shape[0], 128, -1), scales


def unpack4(words, scales):
    return unpack_weight(words.reshape(words.shape[0], 128, -1, 2), scales, "e2m1")


def kspread(k):
    return np.exp2(np.repeat(np.random.randint(-6, 7, k // 32), 32).astype(np.float64))


B, S, HIDDEN, H, HKV, D = 1, 512, 2048, 16, 4, 128
THETA = 10000.0
QS, KVS = H * D, HKV * D
HALF = D // 2


def rope(x):
    freqs = 1.0 / THETA ** (np.arange(0, D, 2) / D)
    ang = np.arange(S)[:, None] * freqs[None, :]
    cos = np.cos(ang)[None, :, None, :]
    sin = np.sin(ang)[None, :, None, :]
    x1, x2 = x[..., :HALF], x[..., HALF:]
    return np.concatenate([x1 * cos - x2 * sin, x1 * sin + x2 * cos], axis=-1)


def setup_inputs():
    s = kspread(HIDDEN)
    hidden_states = np.random.standard_normal((B, S, HIDDEN)) * s
    w = np.random.standard_normal((QS + 2 * KVS, HIDDEN)) * 1.2 / np.sqrt(HIDDEN) / s
    words, scales = pack4(np.ascontiguousarray(w.T))
    hidden_states_words, hidden_states_scales = pack4(np.ascontiguousarray(hidden_states.reshape(B * S, HIDDEN).T))
    return {"hidden_states_words": hidden_states_words,
            "hidden_states_scales": hidden_states_scales,
            "w_qkv_words": words,
            "w_qkv_scales": scales}


def reference(hidden_states_words, hidden_states_scales, w_qkv_words, w_qkv_scales):
    hs = unpack4(hidden_states_words, hidden_states_scales).T.reshape(B, S, HIDDEN)
    qkv = hs @ unpack4(w_qkv_words, w_qkv_scales)
    xq = qkv[..., :QS].reshape(B, S, H, D)
    xk = qkv[..., QS:QS + KVS].reshape(B, S, HKV, D)
    xv = qkv[..., QS + KVS:].reshape(B, S, HKV, D)
    return rope(xq), rope(xk), xv

@@ -1,0 +1,206 @@
+from contextlib import ExitStack
+import math
+
+import concourse.mybir as mybir
+
+F32 = mybir.dt.float32
+I32 = mybir.dt.int32
+BF16 = mybir.dt.bfloat16
+U8 = mybir.dt.uint8
+FP4X4 = mybir.dt.float4_e2m1fn_x4
+ALU = mybir.AluOpType
+ACTF = mybir.ActivationFunctionType
+
+S, HIDDEN, NQKV = 512, 2048, 3072
+FLOPS = 2 * S * HIDDEN * NQKV
+
+P = 128
+PASSES = HIDDEN // 512
+TB = S // P
+NT = 512
+CHUNKS = NQKV // NT
+HALF = 64
+THETA = 10000.0
+
+PLANE_GROUPS = [[0], [1, 2], [3, 4, 5]]
+N_WARM = 10
+LAST_WIDTHS = [256, 128, 128]
+
+
+def tile_gemmaattention_pa_kernel(tc, hs_words, hs_scales, w_words, w_scales, out_q, out_k, out_v):
+    nc = tc.nc
+    q2d = out_q.rearrange("b s h d -> (b s) (h d)")
+    k2d = out_k.rearrange("b s h d -> (b s) (h d)")
+    v2d = out_v.rearrange("b s h d -> (b s) (h d)")
+
+    def dest(c):
+        if c < 4:
+            return q2d[:, NT * c : NT * (c + 1)]
+        return k2d if c == 4 else v2d
+
+    with ExitStack() as ctx:
+        keep = ctx.enter_context(tc.tile_pool(name="keep", bufs=1))
+        work = ctx.enter_context(tc.tile_pool(name="work", bufs=5))
+        psum = ctx.enter_context(tc.psum_pool(name="psum", bufs=8))
+        ctx.enter_context(tc.manual_schedule())
+
+        hs_codes = keep.tile([P, PASSES, 2 * S], U8, name="hs_codes", align_bytes=64)
+        hs_planes = keep.tile([P, PASSES, S], U8, name="hs_planes", align_bytes=64)
+        w_codes = [keep.tile([P, PASSES, 2 * NT], U8, name="w_codes%d" % c, align_bytes=64) for c in range(CHUNKS)]
+        w_planes = [
+            keep.tile([P, PASSES, NT * len(grp)], U8, name="w_planes%d" % i, align_bytes=64)
+            for i, grp in enumerate(PLANE_GROUPS)
+        ]
+
+        def load_codes(tile_ap, words, col0, ncols, g0, g1):
+            nc.sync.dma_start(
+                out=tile_ap[:, g0:g1, :].bitcast(I32),
+                in_=words[g0:g1, :, col0 : col0 + ncols].rearrange("g p n -> p g n").bitcast(I32),
+            )
+
+        def load_scales(planes, scales, col0, ncols):
+            for quad in range(4):
+                nc.sync.dma_start(
+                    out=planes[32 * quad : 32 * quad + 4, :, :].bitcast(I32),
+                    in_=scales[:, 4 * quad : 4 * quad + 4, col0 : col0 + ncols].rearrange("g r n -> r g n").bitcast(I32),
+                )
+
+        pos = keep.tile([P, TB], F32, name="pos")
+        nc.gpsimd.iota(pos[:], pattern=[[P, TB]], base=0, channel_multiplier=1, allow_small_or_imprecise_dtypes=True)
+        zeros = keep.tile([P, NT], BF16, name="zeros")
+        nc.gpsimd.memset(zeros[:], 0.0)
+        idle = psum.tile([P, NT], F32, name="acc")
+        for i in range(N_WARM):
+            nc.tensor.matmul(out=idle[:], lhsT=zeros[:, 0:P], rhs=zeros[:], start=True, stop=True)
+        warm = keep.tile([P, 1], F32, name="warm")
+        nc.scalar.activation(out=warm[:], in_=pos[:, 0:1], func=ACTF.Sin, scale=0.0)
+
+        nc.vector.memset(hs_planes[:].bitcast(I32), 0)
+        nc.vector.memset(w_planes[0][:].bitcast(I32), 0)
+
+        load_codes(hs_codes, hs_words, 0, 2 * S, 0, 1)
+        load_codes(w_codes[0], w_words, 0, 2 * NT, 0, 1)
+        load_scales(hs_planes, hs_scales, 0, S)
+        load_scales(w_planes[0], w_scales, 0, NT)
+        load_codes(hs_codes, hs_words, 0, 2 * S, 1, PASSES)
+        load_codes(w_codes[0], w_words, 0, 2 * NT, 1, PASSES)
+
+        freq = keep.tile([P, 1, HALF], F32, name="freq")
+        ratio = THETA ** (-1.0 / HALF)
+        nc.vector.memset(freq[:, :, 0:1], 1.0)
+        n = 1
+        while n < HALF:
+            nc.vector.tensor_scalar(out=freq[:, :, n : 2 * n], in0=freq[:, :, 0:n], scalar1=ratio ** n,
+                                    scalar2=None, op0=ALU.mult)
+            n *= 2
+        turns = keep.tile([P, 2, TB, HALF], F32, name="turns")
+        for tb in range(TB):
+            nc.vector.tensor_scalar(out=turns[:, 1, tb, :], in0=freq[:, 0, :], scalar1=pos[:, tb : tb + 1],
+                                    scalar2=1.0 / (2.0 * math.pi), op0=ALU.mult, op1=ALU.mult)
+        nc.vector.tensor_scalar(out=turns[:, 0], in0=turns[:, 1], scalar1=0.25, scalar2=None, op0=ALU.add)
+        turns_flat = turns[:].rearrange("p a t d -> p (a t d)")
+        whole = keep.tile([P, 2 * TB * HALF], I32, name="whole")
+        nc.vector.tensor_copy(out=whole[:], in_=turns_flat)
+        frac = keep.tile([P, 2 * TB * HALF], F32, name="frac")
+        nc.vector.tensor_tensor(out=frac[:], in0=turns_flat, in1=whole[:], op=ALU.subtract)
+        negw = keep.tile([P, 2 * TB * HALF], F32, name="negw")
+        nc.vector.scalar_tensor_tensor(out=negw[:], in0=frac[:], scalar=0.5, in1=frac[:], op0=ALU.is_gt,
+                                       op1=ALU.subtract)
+        cossin = keep.tile([P, 2, TB, 1, HALF], F32, name="cossin")
+        nc.scalar.activation(out=cossin[:].rearrange("p a t o d -> p (a t o d)"), in_=negw[:], func=ACTF.Sin,
+                             scale=-2.0 * math.pi)
+        nsin = keep.tile([P, TB, 1, HALF], F32, name="nsin")
+        nc.scalar.activation(out=nsin[:].rearrange("p t o d -> p (t o d)"), in_=negw[:, TB * HALF :], func=ACTF.Sin,
+                             scale=2.0 * math.pi)
+
+        for i in (1, 2):
+            nc.vector.memset(w_planes[i][:].bitcast(I32), 0)
+
+        load_codes(w_codes[1], w_words, 2 * NT * 1, 2 * NT, 0, PASSES)
+        load_codes(w_codes[2], w_words, 2 * NT * 2, 2 * NT, 0, PASSES)
+        load_scales(w_planes[1], w_scales, NT * 1, NT * 2)
+        load_scales(w_planes[2], w_scales, NT * 3, NT * 3)
+        load_codes(w_codes[3], w_words, 2 * NT * 3, 2 * NT, 0, PASSES)
+        load_codes(w_codes[4], w_words, 2 * NT * 4, 2 * NT, 0, PASSES)
+        load_codes(w_codes[5], w_words, 2 * NT * 5, 2 * NT, 0, PASSES)
+
+        plane_of = {}
+        for i, grp in enumerate(PLANE_GROUPS):
+            for j, c in enumerate(grp):
+                plane_of[c] = (i, j)
+
+        def passes(acc, c, tb, col0, ncols, g0=0, g1=PASSES):
+            i, j = plane_of[c]
+            for g in range(g0, g1):
+                nc.tensor.matmul_mx(
+                    out=acc,
+                    lhsT=hs_codes[:, g, 2 * P * tb : 2 * P * (tb + 1)].bitcast(FP4X4),
+                    lhsT_scale=hs_planes[:, g, P * tb : P * (tb + 1)],
+                    rhs=w_codes[c][:, g, 2 * col0 : 2 * (col0 + ncols)].bitcast(FP4X4),
+                    rhs_scale=w_planes[i][:, g, NT * j + col0 : NT * j + col0 + ncols],
+                    start=(g == 0),
+                    stop=(g == PASSES - 1),
+                )
+
+        def products(acc, tb, pt, qt):
+            nc.vector.tensor_tensor(
+                out=pt.rearrange("p (a d) -> p a d", d=HALF),
+                in0=acc.rearrange("p (a d) -> p a d", d=HALF),
+                in1=cossin[:, 0, tb].to_broadcast([P, 8, HALF]),
+                op=ALU.mult,
+            )
+            x4 = acc.rearrange("p (h t d) -> p h t d", t=2, d=HALF)
+            q4 = qt.rearrange("p (h t d) -> p h t d", t=2, d=HALF)
+            nc.vector.tensor_tensor(out=q4[:, :, 1, :], in0=x4[:, :, 0, :],
+                                    in1=cossin[:, 1, tb].to_broadcast([P, 4, HALF]), op=ALU.mult)
+            nc.vector.tensor_tensor(out=q4[:, :, 0, :], in0=x4[:, :, 1, :],
+                                    in1=nsin[:, tb].to_broadcast([P, 4, HALF]), op=ALU.mult)
+
+        late = []
+        first = [psum.tile([P, NT], F32, name="acc") for tb in range(TB)]
+        for tb in range(TB):
+            passes(first[tb][:], 0, tb, 0, NT, 0, 1)
+        for c in range(5):
+            for half in range(2):
+                pt = work.tile([P, 2, NT], F32, name="pt")
+                qt = work.tile([P, 2, NT], F32, name="qt")
+                yt = work.tile([P, 2, NT], F32, name="yt")
+                for j in range(2):
+                    tb = 2 * half + j
+                    if c == 0:
+                        acc = first[tb]
+                        passes(acc[:], c, tb, 0, NT, 1, PASSES)
+                    else:
+                        acc = psum.tile([P, NT], F32, name="acc")
+                        passes(acc[:], c, tb, 0, NT)
+                    products(acc[:], tb, pt[:, j, :], qt[:, j, :])
+                if c < 4:
+                    nc.gpsimd.tensor_tensor(out=yt[:], in0=pt[:], in1=qt[:], op=ALU.add)
+                    nc.sync.dma_start(
+                        out=dest(c)[2 * P * half : 2 * P * (half + 1), :].rearrange("(t p) n -> p t n", p=P),
+                        in_=yt[:],
+                    )
+                else:
+                    late.append((half, pt, qt, yt))
+        for half, pt, qt, yt in late:
+            for j in range(2):
+                tb = 2 * half + j
+                nc.vector.tensor_tensor(out=yt[:, j, :], in0=pt[:, j, :], in1=qt[:, j, :], op=ALU.add)
+                nc.sync.dma_start(out=k2d[P * tb : P * (tb + 1), :], in_=yt[:, j, :])
+
+        for tb in range(TB):
+            vt = work.tile([P, NT], F32, name="vt")
+            if tb < TB - 1:
+                acc = psum.tile([P, NT], F32, name="acc")
+                passes(acc[:], 5, tb, 0, NT)
+                nc.scalar.copy(out=vt[:], in_=acc[:])
+                nc.scalar.dma_start(out=v2d[P * tb : P * (tb + 1), :], in_=vt[:])
+            else:
+                col0 = 0
+                for ncols in LAST_WIDTHS:
+                    acc = psum.tile([P, NT], F32, name="acc")
+                    passes(acc[:, 0:ncols], 5, tb, col0, ncols)
+                    nc.scalar.copy(out=vt[:, col0 : col0 + ncols], in_=acc[:, 0:ncols])
+                    nc.scalar.dma_start(out=v2d[P * tb : P * (tb + 1), col0 : col0 + ncols],
+                                        in_=vt[:, col0 : col0 + ncols])
+                    col0 += ncols

@@ -23,8 +23,8 @@ HALF = 64
 THETA = 10000.0
 
 PLANE_GROUPS = [[0], [1, 2], [3, 4, 5]]
-N_WARM = 10
-LAST_WIDTHS = [256, 128, 128]
+N_WARM = 8
+LAST_WIDTHS = [256, 256]
 
 
 def tile_gemmaattention_pa_kernel(tc, hs_words, hs_scales, w_words, w_scales, out_q, out_k, out_v):
@@ -67,16 +67,18 @@ def tile_gemmaattention_pa_kernel(tc, hs_words, hs_scales, w_words, w_scales, ou
 
         pos = keep.tile([P, TB], F32, name="pos")
         nc.gpsimd.iota(pos[:], pattern=[[P, TB]], base=0, channel_multiplier=1, allow_small_or_imprecise_dtypes=True)
-        zeros = keep.tile([P, NT], BF16, name="zeros")
-        nc.gpsimd.memset(zeros[:], 0.0)
-        idle = psum.tile([P, NT], F32, name="acc")
-        for i in range(N_WARM):
-            nc.tensor.matmul(out=idle[:], lhsT=zeros[:, 0:P], rhs=zeros[:], start=True, stop=True)
         warm = keep.tile([P, 1], F32, name="warm")
         nc.scalar.activation(out=warm[:], in_=pos[:, 0:1], func=ACTF.Sin, scale=0.0)
 
+        one = keep.tile([P, 1], F32, name="one")
+        nc.vector.memset(one[:], 1.0)
         nc.vector.memset(hs_planes[:].bitcast(I32), 0)
         nc.vector.memset(w_planes[0][:].bitcast(I32), 0)
+        zeros = keep.tile([P, NT], BF16, name="zeros")
+        nc.vector.memset(zeros[:], 0.0)
+        idle = psum.tile([P, NT], F32, name="acc")
+        for i in range(N_WARM):
+            nc.tensor.matmul(out=idle[:], lhsT=zeros[:, 0:P], rhs=zeros[:], start=True, stop=True)
 
         load_codes(hs_codes, hs_words, 0, 2 * S, 0, 1)
         load_codes(w_codes[0], w_words, 0, 2 * NT, 0, 1)
@@ -85,40 +87,51 @@ def tile_gemmaattention_pa_kernel(tc, hs_words, hs_scales, w_words, w_scales, ou
         load_codes(hs_codes, hs_words, 0, 2 * S, 1, PASSES)
         load_codes(w_codes[0], w_words, 0, 2 * NT, 1, PASSES)
 
-        freq = keep.tile([P, 1, HALF], F32, name="freq")
         ratio = THETA ** (-1.0 / HALF)
-        nc.vector.memset(freq[:, :, 0:1], 1.0)
-        n = 1
-        while n < HALF:
-            nc.vector.tensor_scalar(out=freq[:, :, n : 2 * n], in0=freq[:, :, 0:n], scalar1=ratio ** n,
+        freq = keep.tile([P, HALF], F32, name="freq")
+        for k in range(4):
+            nc.vector.tensor_scalar(out=freq[:, k : k + 1], in0=one[:], scalar1=ratio ** k / (2.0 * math.pi),
                                     scalar2=None, op0=ALU.mult)
-            n *= 2
-        turns = keep.tile([P, 2, TB, HALF], F32, name="turns")
-        for tb in range(TB):
-            nc.vector.tensor_scalar(out=turns[:, 1, tb, :], in0=freq[:, 0, :], scalar1=pos[:, tb : tb + 1],
-                                    scalar2=1.0 / (2.0 * math.pi), op0=ALU.mult, op1=ALU.mult)
-        nc.vector.tensor_scalar(out=turns[:, 0], in0=turns[:, 1], scalar1=0.25, scalar2=None, op0=ALU.add)
-        turns_flat = turns[:].rearrange("p a t d -> p (a t d)")
-        whole = keep.tile([P, 2 * TB * HALF], I32, name="whole")
-        nc.vector.tensor_copy(out=whole[:], in_=turns_flat)
-        frac = keep.tile([P, 2 * TB * HALF], F32, name="frac")
-        nc.vector.tensor_tensor(out=frac[:], in0=turns_flat, in1=whole[:], op=ALU.subtract)
-        negw = keep.tile([P, 2 * TB * HALF], F32, name="negw")
-        nc.vector.scalar_tensor_tensor(out=negw[:], in0=frac[:], scalar=0.5, in1=frac[:], op0=ALU.is_gt,
-                                       op1=ALU.subtract)
-        cossin = keep.tile([P, 2, TB, 1, HALF], F32, name="cossin")
-        nc.scalar.activation(out=cossin[:].rearrange("p a t o d -> p (a t o d)"), in_=negw[:], func=ACTF.Sin,
-                             scale=-2.0 * math.pi)
-        nsin = keep.tile([P, TB, 1, HALF], F32, name="nsin")
-        nc.scalar.activation(out=nsin[:].rearrange("p t o d -> p (t o d)"), in_=negw[:, TB * HALF :], func=ACTF.Sin,
-                             scale=2.0 * math.pi)
+        nc.vector.memset(w_planes[1][:, 0:2, :].bitcast(I32), 0)
+        for j in range(1, 4):
+            nc.vector.tensor_scalar(out=freq[:, 4 * j : 4 * j + 4], in0=freq[:, 0:4], scalar1=ratio ** (4 * j),
+                                    scalar2=None, op0=ALU.mult)
+        nc.vector.memset(w_planes[1][:, 2:4, :].bitcast(I32), 0)
+        for j in range(1, 4):
+            nc.vector.tensor_scalar(out=freq[:, 16 * j : 16 * j + 16], in0=freq[:, 0:16], scalar1=ratio ** (16 * j),
+                                    scalar2=None, op0=ALU.mult)
+        nc.vector.memset(w_planes[2][:, 0:1, :].bitcast(I32), 0)
 
-        for i in (1, 2):
-            nc.vector.memset(w_planes[i][:].bitcast(I32), 0)
-
+        load_scales(w_planes[1], w_scales, NT * 1, NT * 2)
         load_codes(w_codes[1], w_words, 2 * NT * 1, 2 * NT, 0, PASSES)
         load_codes(w_codes[2], w_words, 2 * NT * 2, 2 * NT, 0, PASSES)
-        load_scales(w_planes[1], w_scales, NT * 1, NT * 2)
+
+        turns = keep.tile([P, 2, TB, HALF], F32, name="turns")
+        for a in range(2):
+            for tb in range(TB):
+                nc.vector.tensor_scalar(out=turns[:, a, tb, :], in0=freq[:], scalar1=pos[:, tb : tb + 1],
+                                        scalar2=0.25 * (1 - a), op0=ALU.mult, op1=ALU.add)
+        turns2 = turns[:].rearrange("p a t d -> p a (t d)")
+        whole = keep.tile([P, 2, TB * HALF], I32, name="whole")
+        frac = keep.tile([P, 2, TB * HALF], F32, name="frac")
+        negw = keep.tile([P, 2, TB * HALF], F32, name="negw")
+        for a in range(2):
+            nc.vector.tensor_copy(out=whole[:, a, :], in_=turns2[:, a, :])
+        for a in range(2):
+            nc.vector.tensor_tensor(out=frac[:, a, :], in0=turns2[:, a, :], in1=whole[:, a, :], op=ALU.subtract)
+        for a in range(2):
+            nc.vector.scalar_tensor_tensor(out=negw[:, a, :], in0=frac[:, a, :], scalar=0.5, in1=frac[:, a, :],
+                                           op0=ALU.is_gt, op1=ALU.subtract)
+        cossin = keep.tile([P, 2, TB, 1, HALF], F32, name="cossin")
+        for a in range(2):
+            nc.scalar.activation(out=cossin[:, a].rearrange("p t o d -> p (t o d)"), in_=negw[:, a, :], func=ACTF.Sin,
+                                 scale=-2.0 * math.pi)
+        nsin = keep.tile([P, TB, 1, HALF], F32, name="nsin")
+        nc.scalar.activation(out=nsin[:].rearrange("p t o d -> p (t o d)"), in_=negw[:, 1, :], func=ACTF.Sin,
+                             scale=2.0 * math.pi)
+
+        nc.vector.memset(w_planes[2][:, 1:4, :].bitcast(I32), 0)
+
         load_scales(w_planes[2], w_scales, NT * 3, NT * 3)
         load_codes(w_codes[3], w_words, 2 * NT * 3, 2 * NT, 0, PASSES)
         load_codes(w_codes[4], w_words, 2 * NT * 4, 2 * NT, 0, PASSES)
@@ -183,10 +196,11 @@ def tile_gemmaattention_pa_kernel(tc, hs_words, hs_scales, w_words, w_scales, ou
                 else:
                     late.append((half, pt, qt, yt))
         for half, pt, qt, yt in late:
-            for j in range(2):
-                tb = 2 * half + j
-                nc.vector.tensor_tensor(out=yt[:, j, :], in0=pt[:, j, :], in1=qt[:, j, :], op=ALU.add)
-                nc.sync.dma_start(out=k2d[P * tb : P * (tb + 1), :], in_=yt[:, j, :])
+            nc.vector.tensor_tensor(out=yt[:], in0=pt[:], in1=qt[:], op=ALU.add)
+            nc.sync.dma_start(
+                out=k2d[2 * P * half : 2 * P * (half + 1), :].rearrange("(t p) n -> p t n", p=P),
+                in_=yt[:],
+            )
 
         for tb in range(TB):
             vt = work.tile([P, NT], F32, name="vt")

@@ -80,10 +80,10 @@ def tile_gemmaattention_pa_kernel(tc, hs_words, hs_scales, w_words, w_scales, ou
         for i in range(N_WARM):
             nc.tensor.matmul(out=idle[:], lhsT=zeros[:, 0:P], rhs=zeros[:], start=True, stop=True)
 
-        load_codes(hs_codes, hs_words, 0, 2 * S, 0, 1)
-        load_codes(w_codes[0], w_words, 0, 2 * NT, 0, 1)
         load_scales(hs_planes, hs_scales, 0, S)
         load_scales(w_planes[0], w_scales, 0, NT)
+        load_codes(hs_codes, hs_words, 0, 2 * S, 0, 1)
+        load_codes(w_codes[0], w_words, 0, 2 * NT, 0, 1)
         load_codes(hs_codes, hs_words, 0, 2 * S, 1, PASSES)
         load_codes(w_codes[0], w_words, 0, 2 * NT, 1, PASSES)
 

@@ -23,7 +23,7 @@ HALF = 64
 THETA = 10000.0
 
 PLANE_GROUPS = [[0], [1, 2], [3, 4, 5]]
-N_WARM = 8
+N_WARM = 10
 LAST_WIDTHS = [256, 256]
 
 
@@ -80,10 +80,10 @@ def tile_gemmaattention_pa_kernel(tc, hs_words, hs_scales, w_words, w_scales, ou
         for i in range(N_WARM):
             nc.tensor.matmul(out=idle[:], lhsT=zeros[:, 0:P], rhs=zeros[:], start=True, stop=True)
 
-        load_scales(hs_planes, hs_scales, 0, S)
-        load_scales(w_planes[0], w_scales, 0, NT)
         load_codes(hs_codes, hs_words, 0, 2 * S, 0, 1)
         load_codes(w_codes[0], w_words, 0, 2 * NT, 0, 1)
+        load_scales(hs_planes, hs_scales, 0, S)
+        load_scales(w_planes[0], w_scales, 0, NT)
         load_codes(hs_codes, hs_words, 0, 2 * S, 1, PASSES)
         load_codes(w_codes[0], w_words, 0, 2 * NT, 1, PASSES)
 

@@ -122,13 +122,10 @@ def tile_gemmaattention_pa_kernel(tc, hs_words, hs_scales, w_words, w_scales, ou
         for a in range(2):
             nc.vector.scalar_tensor_tensor(out=negw[:, a, :], in0=frac[:, a, :], scalar=0.5, in1=frac[:, a, :],
                                            op0=ALU.is_gt, op1=ALU.subtract)
-        cossin = keep.tile([P, 2, TB, 1, HALF], F32, name="cossin")
-        for a in range(2):
-            nc.scalar.activation(out=cossin[:, a].rearrange("p t o d -> p (t o d)"), in_=negw[:, a, :], func=ACTF.Sin,
-                                 scale=-2.0 * math.pi)
-        nsin = keep.tile([P, TB, 1, HALF], F32, name="nsin")
-        nc.scalar.activation(out=nsin[:].rearrange("p t o d -> p (t o d)"), in_=negw[:, 1, :], func=ACTF.Sin,
-                             scale=2.0 * math.pi)
+        rot = keep.tile([P, TB, 2, 2, HALF], F32, name="rot")
+        for u, t, a, sign in ((0, 0, 0, -1.0), (0, 1, 1, 1.0), (1, 0, 1, -1.0), (1, 1, 0, -1.0)):
+            nc.scalar.activation(out=rot[:, :, u, t, :], in_=negw[:, a, :].rearrange("p (b d) -> p b d", d=HALF),
+                                 func=ACTF.Sin, scale=sign * 2.0 * math.pi)
 
         nc.vector.memset(w_planes[2][:, 1:4, :].bitcast(I32), 0)
 
@@ -155,19 +152,18 @@ def tile_gemmaattention_pa_kernel(tc, hs_words, hs_scales, w_words, w_scales, ou
                     stop=(g == PASSES - 1),
                 )
 
-        def products(acc, tb, pt, qt):
+        def products(acc, tb, et):
             nc.vector.tensor_tensor(
-                out=pt.rearrange("p (a d) -> p a d", d=HALF),
-                in0=acc.rearrange("p (a d) -> p a d", d=HALF),
-                in1=cossin[:, 0, tb].to_broadcast([P, 8, HALF]),
+                out=et.rearrange("p u (h c) -> p u h c", c=2 * HALF),
+                in0=acc.unsqueeze(1).to_broadcast([P, 2, NT]).rearrange("p u (h c) -> p u h c", c=2 * HALF),
+                in1=rot[:, tb].rearrange("p u t d -> p u (t d)").unsqueeze(2).to_broadcast([P, 2, 4, 2 * HALF]),
                 op=ALU.mult,
             )
-            x4 = acc.rearrange("p (h t d) -> p h t d", t=2, d=HALF)
-            q4 = qt.rearrange("p (h t d) -> p h t d", t=2, d=HALF)
-            nc.vector.tensor_tensor(out=q4[:, :, 1, :], in0=x4[:, :, 0, :],
-                                    in1=cossin[:, 1, tb].to_broadcast([P, 4, HALF]), op=ALU.mult)
-            nc.vector.tensor_tensor(out=q4[:, :, 0, :], in0=x4[:, :, 1, :],
-                                    in1=nsin[:, tb].to_broadcast([P, 4, HALF]), op=ALU.mult)
+
+        def add_halves(engine, yt, et):
+            e5 = et.rearrange("p u j (h t d) -> p (j h) u t d", t=2, d=HALF)
+            engine.tensor_tensor(out=yt.rearrange("p j (h u d) -> p (j h) u d", u=2, d=HALF),
+                                 in0=e5[:, :, :, 0, :], in1=e5[:, :, :, 1, :], op=ALU.add)
 
         late = []
         first = [psum.tile([P, NT], F32, name="acc") for tb in range(TB)]
@@ -175,8 +171,7 @@ def tile_gemmaattention_pa_kernel(tc, hs_words, hs_scales, w_words, w_scales, ou
             passes(first[tb][:], 0, tb, 0, NT, 0, 1)
         for c in range(5):
             for half in range(2):
-                pt = work.tile([P, 2, NT], F32, name="pt")
-                qt = work.tile([P, 2, NT], F32, name="qt")
+                et = work.tile([P, 2, 2, NT], F32, name="et")
                 yt = work.tile([P, 2, NT], F32, name="yt")
                 for j in range(2):
                     tb = 2 * half + j
@@ -186,17 +181,17 @@ def tile_gemmaattention_pa_kernel(tc, hs_words, hs_scales, w_words, w_scales, ou
                     else:
                         acc = psum.tile([P, NT], F32, name="acc")
                         passes(acc[:], c, tb, 0, NT)
-                    products(acc[:], tb, pt[:, j, :], qt[:, j, :])
+                    products(acc[:], tb, et[:, :, j, :])
                 if c < 4:
-                    nc.gpsimd.tensor_tensor(out=yt[:], in0=pt[:], in1=qt[:], op=ALU.add)
+                    add_halves(nc.gpsimd, yt[:], et[:])
                     nc.sync.dma_start(
                         out=dest(c)[2 * P * half : 2 * P * (half + 1), :].rearrange("(t p) n -> p t n", p=P),
                         in_=yt[:],
                     )
                 else:
-                    late.append((half, pt, qt, yt))
-        for half, pt, qt, yt in late:
-            nc.vector.tensor_tensor(out=yt[:], in0=pt[:], in1=qt[:], op=ALU.add)
+                    late.append((half, et, yt))
+        for half, et, yt in late:
+            add_halves(nc.vector, yt[:], et[:])
             nc.sync.dma_start(
                 out=k2d[2 * P * half : 2 * P * (half + 1), :].rearrange("(t p) n -> p t n", p=P),
                 in_=yt[:],

@@ -25,6 +25,8 @@ THETA = 10000.0
 PLANE_GROUPS = [[0], [1, 2], [3, 4, 5]]
 N_WARM = 10
 LAST_WIDTHS = [256, 256]
+V_AFTER = {3: [0, 1]}
+V_LAST = [2, 3]
 
 
 def tile_gemmaattention_pa_kernel(tc, hs_words, hs_scales, w_words, w_scales, out_q, out_k, out_v):
@@ -165,6 +167,16 @@ def tile_gemmaattention_pa_kernel(tc, hs_words, hs_scales, w_words, w_scales, ou
             engine.tensor_tensor(out=yt.rearrange("p j (h u d) -> p (j h) u d", u=2, d=HALF),
                                  in0=e5[:, :, :, 0, :], in1=e5[:, :, :, 1, :], op=ALU.add)
 
+        def values(tb, widths):
+            vt = work.tile([P, NT], F32, name="vt")
+            col0 = 0
+            for ncols in widths:
+                acc = psum.tile([P, NT], F32, name="acc")
+                passes(acc[:, 0:ncols], 5, tb, col0, ncols)
+                nc.scalar.copy(out=vt[:, col0 : col0 + ncols], in_=acc[:, 0:ncols])
+                col0 += ncols
+                nc.scalar.dma_start(out=v2d[P * tb : P * (tb + 1), col0 - ncols : col0], in_=vt[:, col0 - ncols : col0])
+
         late = []
         first = [psum.tile([P, NT], F32, name="acc") for tb in range(TB)]
         for tb in range(TB):
@@ -182,34 +194,24 @@ def tile_gemmaattention_pa_kernel(tc, hs_words, hs_scales, w_words, w_scales, ou
                         acc = psum.tile([P, NT], F32, name="acc")
                         passes(acc[:], c, tb, 0, NT)
                     products(acc[:], tb, et[:, :, j, :])
-                if c < 4:
+                    if (c == 4 or c == 0) and half == 0:
+                        add_halves(nc.gpsimd, yt[:, j : j + 1, :], et[:, :, j : j + 1, :])
+                        nc.sync.dma_start(out=dest(c)[P * tb : P * (tb + 1), :], in_=yt[:, j, :])
+                if 0 < c < 4 or (c == 0 and half == 1):
                     add_halves(nc.gpsimd, yt[:], et[:])
                     nc.sync.dma_start(
                         out=dest(c)[2 * P * half : 2 * P * (half + 1), :].rearrange("(t p) n -> p t n", p=P),
                         in_=yt[:],
                     )
-                else:
+                elif half == 1:
                     late.append((half, et, yt))
+            for tb in V_AFTER.get(c, []):
+                values(tb, [NT])
         for half, et, yt in late:
-            add_halves(nc.vector, yt[:], et[:])
-            nc.sync.dma_start(
-                out=k2d[2 * P * half : 2 * P * (half + 1), :].rearrange("(t p) n -> p t n", p=P),
-                in_=yt[:],
-            )
-
-        for tb in range(TB):
-            vt = work.tile([P, NT], F32, name="vt")
-            if tb < TB - 1:
-                acc = psum.tile([P, NT], F32, name="acc")
-                passes(acc[:], 5, tb, 0, NT)
-                nc.scalar.copy(out=vt[:], in_=acc[:])
-                nc.scalar.dma_start(out=v2d[P * tb : P * (tb + 1), :], in_=vt[:])
-            else:
-                col0 = 0
-                for ncols in LAST_WIDTHS:
-                    acc = psum.tile([P, NT], F32, name="acc")
-                    passes(acc[:, 0:ncols], 5, tb, col0, ncols)
-                    nc.scalar.copy(out=vt[:, col0 : col0 + ncols], in_=acc[:, 0:ncols])
-                    nc.scalar.dma_start(out=v2d[P * tb : P * (tb + 1), col0 : col0 + ncols],
-                                        in_=vt[:, col0 : col0 + ncols])
-                    col0 += ncols
+            for j in range(2):
+                tb = 2 * half + j
+                add_halves(nc.vector, yt[:, j : j + 1, :], et[:, :, j : j + 1, :])
+                nc.sync.dma_start(out=k2d[P * tb : P * (tb + 1), :], in_=yt[:, j, :])
+        for tb in V_LAST[:-1]:
+            values(tb, [NT])
+        values(V_LAST[-1], LAST_WIDTHS)

@@ -25,8 +25,8 @@ THETA = 10000.0
 PLANE_GROUPS = [[0], [1, 2], [3, 4, 5]]
 N_WARM = 10
 LAST_WIDTHS = [256, 256]
-V_AFTER = {3: [0, 1]}
-V_LAST = [2, 3]
+V_AFTER = {3: [0, 1, 2]}
+V_LAST = [3]
 
 
 def tile_gemmaattention_pa_kernel(tc, hs_words, hs_scales, w_words, w_scales, out_q, out_k, out_v):

@@ -61,10 +61,10 @@ def tile_gemmaattention_pa_kernel(tc, hs_words, hs_scales, w_words, w_scales, ou
             )
 
         def load_scales(planes, scales, col0, ncols):
-            for quad in range(4):
+            for r in range(4):
                 nc.sync.dma_start(
-                    out=planes[32 * quad : 32 * quad + 4, :, :].bitcast(I32),
-                    in_=scales[:, 4 * quad : 4 * quad + 4, col0 : col0 + ncols].rearrange("g r n -> r g n").bitcast(I32),
+                    out=planes[r : P : 32, :, :].bitcast(I32),
+                    in_=scales[:, r : 16 : 4, col0 : col0 + ncols].rearrange("g q n -> q g n").bitcast(I32),
                 )
 
         pos = keep.tile([P, TB], F32, name="pos")

@@ -197,21 +197,23 @@ def tile_gemmaattention_pa_kernel(tc, hs_words, hs_scales, w_words, w_scales, ou
                     if (c == 4 or c == 0) and half == 0:
                         add_halves(nc.gpsimd, yt[:, j : j + 1, :], et[:, :, j : j + 1, :])
                         nc.sync.dma_start(out=dest(c)[P * tb : P * (tb + 1), :], in_=yt[:, j, :])
-                if 0 < c < 4 or (c == 0 and half == 1):
+                if 0 < c < 3 or (c == 0 and half == 1):
                     add_halves(nc.gpsimd, yt[:], et[:])
                     nc.sync.dma_start(
                         out=dest(c)[2 * P * half : 2 * P * (half + 1), :].rearrange("(t p) n -> p t n", p=P),
                         in_=yt[:],
                     )
-                elif half == 1:
+                elif c == 3 or half == 1:
                     late.append((half, et, yt))
+            if c >= 3:
+                for half, et, yt in late:
+                    for j in range(2):
+                        tb = 2 * half + j
+                        add_halves(nc.vector, yt[:, j : j + 1, :], et[:, :, j : j + 1, :])
+                        nc.sync.dma_start(out=dest(c)[P * tb : P * (tb + 1), :], in_=yt[:, j, :])
+                late = []
             for tb in V_AFTER.get(c, []):
                 values(tb, [NT])
-        for half, et, yt in late:
-            for j in range(2):
-                tb = 2 * half + j
-                add_halves(nc.vector, yt[:, j : j + 1, :], et[:, :, j : j + 1, :])
-                nc.sync.dma_start(out=k2d[P * tb : P * (tb + 1), :], in_=yt[:, j, :])
         for tb in V_LAST[:-1]:
             values(tb, [NT])
         values(V_LAST[-1], LAST_WIDTHS)

@@ -109,25 +109,28 @@ def tile_gemmaattention_pa_kernel(tc, hs_words, hs_scales, w_words, w_scales, ou
         load_codes(w_codes[2], w_words, 2 * NT * 2, 2 * NT, 0, PASSES)
 
         turns = keep.tile([P, 2, TB, HALF], F32, name="turns")
-        for a in range(2):
-            for tb in range(TB):
-                nc.vector.tensor_scalar(out=turns[:, a, tb, :], in0=freq[:], scalar1=pos[:, tb : tb + 1],
-                                        scalar2=0.25 * (1 - a), op0=ALU.mult, op1=ALU.add)
-        turns2 = turns[:].rearrange("p a t d -> p a (t d)")
-        whole = keep.tile([P, 2, TB * HALF], I32, name="whole")
-        frac = keep.tile([P, 2, TB * HALF], F32, name="frac")
-        negw = keep.tile([P, 2, TB * HALF], F32, name="negw")
-        for a in range(2):
-            nc.vector.tensor_copy(out=whole[:, a, :], in_=turns2[:, a, :])
-        for a in range(2):
-            nc.vector.tensor_tensor(out=frac[:, a, :], in0=turns2[:, a, :], in1=whole[:, a, :], op=ALU.subtract)
-        for a in range(2):
-            nc.vector.scalar_tensor_tensor(out=negw[:, a, :], in0=frac[:, a, :], scalar=0.5, in1=frac[:, a, :],
-                                           op0=ALU.is_gt, op1=ALU.subtract)
+        nc.vector.tensor_tensor(out=turns[:, 1], in0=freq[:].unsqueeze(1).to_broadcast([P, TB, HALF]),
+                                in1=pos[:].unsqueeze(2).to_broadcast([P, TB, HALF]), op=ALU.mult)
+        nc.vector.tensor_scalar(out=turns[:, 0], in0=turns[:, 1], scalar1=0.25, scalar2=None, op0=ALU.add)
+        whole = keep.tile([P, 2, TB, HALF], I32, name="whole")
+        frac = keep.tile([P, 2, TB, HALF], F32, name="frac")
+        for a in (1, 0):
+            nc.vector.tensor_copy(out=whole[:, a], in_=turns[:, a])
+        for a in (1, 0):
+            nc.vector.tensor_tensor(out=frac[:, a], in0=turns[:, a], in1=whole[:, a], op=ALU.subtract)
+        sin_w = keep.tile([P, TB, 2, HALF], F32, name="sin_w")
+        cos_w = keep.tile([P, TB, 1, HALF], F32, name="cos_w")
+        nc.vector.scalar_tensor_tensor(out=sin_w[:, :, 1, :], in0=frac[:, 1], scalar=0.5, in1=frac[:, 1],
+                                       op0=ALU.is_gt, op1=ALU.subtract)
+        nc.vector.scalar_tensor_tensor(out=cos_w[:, :, 0, :], in0=frac[:, 0], scalar=0.5, in1=frac[:, 0],
+                                       op0=ALU.is_gt, op1=ALU.subtract)
+        nc.vector.tensor_scalar(out=sin_w[:, :, 0, :], in0=sin_w[:, :, 1, :], scalar1=-1.0, scalar2=None, op0=ALU.mult)
         rot = keep.tile([P, TB, 2, 2, HALF], F32, name="rot")
-        for u, t, a, sign in ((0, 0, 0, -1.0), (0, 1, 1, 1.0), (1, 0, 1, -1.0), (1, 1, 0, -1.0)):
-            nc.scalar.activation(out=rot[:, :, u, t, :], in_=negw[:, a, :].rearrange("p (b d) -> p b d", d=HALF),
-                                 func=ACTF.Sin, scale=sign * 2.0 * math.pi)
+        slots = rot[:].rearrange("p b u t d -> p b (u t) d")
+        for tb in range(TB):
+            nc.scalar.activation(out=slots[:, tb, 0:4:3, :], in_=cos_w[:, tb].to_broadcast([P, 2, HALF]), func=ACTF.Sin,
+                                 scale=-2.0 * math.pi)
+            nc.scalar.activation(out=slots[:, tb, 1:3, :], in_=sin_w[:, tb], func=ACTF.Sin, scale=-2.0 * math.pi)
 
         nc.vector.memset(w_planes[2][:, 1:4, :].bitcast(I32), 0)
 

@@ -104,8 +104,8 @@ def tile_gemmaattention_pa_kernel(tc, hs_words, hs_scales, w_words, w_scales, ou
                                     scalar2=None, op0=ALU.mult)
         nc.vector.memset(w_planes[2][:, 0:1, :].bitcast(I32), 0)
 
-        load_scales(w_planes[1], w_scales, NT * 1, NT * 2)
         load_codes(w_codes[1], w_words, 2 * NT * 1, 2 * NT, 0, PASSES)
+        load_scales(w_planes[1], w_scales, NT * 1, NT * 2)
         load_codes(w_codes[2], w_words, 2 * NT * 2, 2 * NT, 0, PASSES)
 
         turns = keep.tile([P, 2, TB, HALF], F32, name="turns")

@@ -46,11 +46,11 @@ def tile_gemmaattention_pa_kernel(tc, hs_words, hs_scales, w_words, w_scales, ou
         psum = ctx.enter_context(tc.psum_pool(name="psum", bufs=8))
         ctx.enter_context(tc.manual_schedule())
 
-        hs_codes = keep.tile([P, PASSES, 2 * S], U8, name="hs_codes", align_bytes=64)
-        hs_planes = keep.tile([P, PASSES, S], U8, name="hs_planes", align_bytes=64)
-        w_codes = [keep.tile([P, PASSES, 2 * NT], U8, name="w_codes%d" % c, align_bytes=64) for c in range(CHUNKS)]
+        hs_codes = keep.tile([P, PASSES, 2 * S], U8, name="hs_codes", align_bytes=256)
+        hs_planes = keep.tile([P, PASSES, S], U8, name="hs_planes", align_bytes=256)
+        w_codes = [keep.tile([P, PASSES, 2 * NT], U8, name="w_codes%d" % c, align_bytes=256) for c in range(CHUNKS)]
         w_planes = [
-            keep.tile([P, PASSES, NT * len(grp)], U8, name="w_planes%d" % i, align_bytes=64)
+            keep.tile([P, PASSES, NT * len(grp)], U8, name="w_planes%d" % i, align_bytes=256)
             for i, grp in enumerate(PLANE_GROUPS)
         ]
 

@@ -171,7 +171,7 @@ def tile_gemmaattention_pa_kernel(tc, hs_words, hs_scales, w_words, w_scales, ou
                                  in0=e5[:, :, :, 0, :], in1=e5[:, :, :, 1, :], op=ALU.add)
 
         def values(tb, widths):
-            vt = work.tile([P, NT], F32, name="vt")
+            vt = work.tile([P, NT], F32, name="vt", align_bytes=256)
             col0 = 0
             for ncols in widths:
                 acc = psum.tile([P, NT], F32, name="acc")
@@ -186,8 +186,8 @@ def tile_gemmaattention_pa_kernel(tc, hs_words, hs_scales, w_words, w_scales, ou
             passes(first[tb][:], 0, tb, 0, NT, 0, 1)
         for c in range(5):
             for half in range(2):
-                et = work.tile([P, 2, 2, NT], F32, name="et")
-                yt = work.tile([P, 2, NT], F32, name="yt")
+                et = work.tile([P, 2, 2, NT], F32, name="et", align_bytes=256)
+                yt = work.tile([P, 2, NT], F32, name="yt", align_bytes=256)
                 for j in range(2):
                     tb = 2 * half + j
                     if c == 0:

from contextlib import ExitStack
import math

import concourse.mybir as mybir

F32 = mybir.dt.float32
I32 = mybir.dt.int32
BF16 = mybir.dt.bfloat16
U8 = mybir.dt.uint8
FP4X4 = mybir.dt.float4_e2m1fn_x4
ALU = mybir.AluOpType
ACTF = mybir.ActivationFunctionType

S, HIDDEN, NQKV = 512, 2048, 3072
FLOPS = 2 * S * HIDDEN * NQKV

P = 128
PASSES = HIDDEN // 512
TB = S // P
NT = 512
CHUNKS = NQKV // NT
HALF = 64
THETA = 10000.0

PLANE_GROUPS = [[0], [1, 2], [3, 4, 5]]
N_WARM = 10
LAST_WIDTHS = [256, 256]
V_AFTER = {3: [0, 1, 2]}
V_LAST = [3]


def tile_gemmaattention_pa_kernel(tc, hs_words, hs_scales, w_words, w_scales, out_q, out_k, out_v):
    nc = tc.nc
    q2d = out_q.rearrange("b s h d -> (b s) (h d)")
    k2d = out_k.rearrange("b s h d -> (b s) (h d)")
    v2d = out_v.rearrange("b s h d -> (b s) (h d)")

    def dest(c):
        if c < 4:
            return q2d[:, NT * c : NT * (c + 1)]
        return k2d if c == 4 else v2d

    with ExitStack() as ctx:
        keep = ctx.enter_context(tc.tile_pool(name="keep", bufs=1))
        work = ctx.enter_context(tc.tile_pool(name="work", bufs=5))
        psum = ctx.enter_context(tc.psum_pool(name="psum", bufs=8))
        ctx.enter_context(tc.manual_schedule())

        hs_codes = keep.tile([P, PASSES, 2 * S], U8, name="hs_codes", align_bytes=256)
        hs_planes = keep.tile([P, PASSES, S], U8, name="hs_planes", align_bytes=256)
        w_codes = [keep.tile([P, PASSES, 2 * NT], U8, name="w_codes%d" % c, align_bytes=256) for c in range(CHUNKS)]
        w_planes = [
            keep.tile([P, PASSES, NT * len(grp)], U8, name="w_planes%d" % i, align_bytes=256)
            for i, grp in enumerate(PLANE_GROUPS)
        ]

        def load_codes(tile_ap, words, col0, ncols, g0, g1):
            nc.sync.dma_start(
                out=tile_ap[:, g0:g1, :].bitcast(I32),
                in_=words[g0:g1, :, col0 : col0 + ncols].rearrange("g p n -> p g n").bitcast(I32),
            )

        def load_scales(planes, scales, col0, ncols):
            for r in range(4):
                nc.sync.dma_start(
                    out=planes[r : P : 32, :, :].bitcast(I32),
                    in_=scales[:, r : 16 : 4, col0 : col0 + ncols].rearrange("g q n -> q g n").bitcast(I32),
                )

        pos = keep.tile([P, TB], F32, name="pos")
        nc.gpsimd.iota(pos[:], pattern=[[P, TB]], base=0, channel_multiplier=1, allow_small_or_imprecise_dtypes=True)
        warm = keep.tile([P, 1], F32, name="warm")
        nc.scalar.activation(out=warm[:], in_=pos[:, 0:1], func=ACTF.Sin, scale=0.0)

        one = keep.tile([P, 1], F32, name="one")
        nc.vector.memset(one[:], 1.0)
        nc.vector.memset(hs_planes[:].bitcast(I32), 0)
        nc.vector.memset(w_planes[0][:].bitcast(I32), 0)
        zeros = keep.tile([P, NT], BF16, name="zeros")
        nc.vector.memset(zeros[:], 0.0)
        idle = psum.tile([P, NT], F32, name="acc")
        for i in range(N_WARM):
            nc.tensor.matmul(out=idle[:], lhsT=zeros[:, 0:P], rhs=zeros[:], start=True, stop=True)

        load_codes(hs_codes, hs_words, 0, 2 * S, 0, 1)
        load_codes(w_codes[0], w_words, 0, 2 * NT, 0, 1)
        load_scales(hs_planes, hs_scales, 0, S)
        load_scales(w_planes[0], w_scales, 0, NT)
        load_codes(hs_codes, hs_words, 0, 2 * S, 1, PASSES)
        load_codes(w_codes[0], w_words, 0, 2 * NT, 1, PASSES)

        ratio = THETA ** (-1.0 / HALF)
        freq = keep.tile([P, HALF], F32, name="freq")
        for k in range(4):
            nc.vector.tensor_scalar(out=freq[:, k : k + 1], in0=one[:], scalar1=ratio ** k / (2.0 * math.pi),
                                    scalar2=None, op0=ALU.mult)
        nc.vector.memset(w_planes[1][:, 0:2, :].bitcast(I32), 0)
        for j in range(1, 4):
            nc.vector.tensor_scalar(out=freq[:, 4 * j : 4 * j + 4], in0=freq[:, 0:4], scalar1=ratio ** (4 * j),
                                    scalar2=None, op0=ALU.mult)
        nc.vector.memset(w_planes[1][:, 2:4, :].bitcast(I32), 0)
        for j in range(1, 4):
            nc.vector.tensor_scalar(out=freq[:, 16 * j : 16 * j + 16], in0=freq[:, 0:16], scalar1=ratio ** (16 * j),
                                    scalar2=None, op0=ALU.mult)
        nc.vector.memset(w_planes[2][:, 0:1, :].bitcast(I32), 0)

        load_codes(w_codes[1], w_words, 2 * NT * 1, 2 * NT, 0, PASSES)
        load_scales(w_planes[1], w_scales, NT * 1, NT * 2)
        load_codes(w_codes[2], w_words, 2 * NT * 2, 2 * NT, 0, PASSES)

        turns = keep.tile([P, 2, TB, HALF], F32, name="turns")
        nc.vector.tensor_tensor(out=turns[:, 1], in0=freq[:].unsqueeze(1).to_broadcast([P, TB, HALF]),
                                in1=pos[:].unsqueeze(2).to_broadcast([P, TB, HALF]), op=ALU.mult)
        nc.vector.tensor_scalar(out=turns[:, 0], in0=turns[:, 1], scalar1=0.25, scalar2=None, op0=ALU.add)
        whole = keep.tile([P, 2, TB, HALF], I32, name="whole")
        frac = keep.tile([P, 2, TB, HALF], F32, name="frac")
        for a in (1, 0):
            nc.vector.tensor_copy(out=whole[:, a], in_=turns[:, a])
        for a in (1, 0):
            nc.vector.tensor_tensor(out=frac[:, a], in0=turns[:, a], in1=whole[:, a], op=ALU.subtract)
        sin_w = keep.tile([P, TB, 2, HALF], F32, name="sin_w")
        cos_w = keep.tile([P, TB, 1, HALF], F32, name="cos_w")
        nc.vector.scalar_tensor_tensor(out=sin_w[:, :, 1, :], in0=frac[:, 1], scalar=0.5, in1=frac[:, 1],
                                       op0=ALU.is_gt, op1=ALU.subtract)
        nc.vector.scalar_tensor_tensor(out=cos_w[:, :, 0, :], in0=frac[:, 0], scalar=0.5, in1=frac[:, 0],
                                       op0=ALU.is_gt, op1=ALU.subtract)
        nc.vector.tensor_scalar(out=sin_w[:, :, 0, :], in0=sin_w[:, :, 1, :], scalar1=-1.0, scalar2=None, op0=ALU.mult)
        rot = keep.tile([P, TB, 2, 2, HALF], F32, name="rot")
        slots = rot[:].rearrange("p b u t d -> p b (u t) d")
        for tb in range(TB):
            nc.scalar.activation(out=slots[:, tb, 0:4:3, :], in_=cos_w[:, tb].to_broadcast([P, 2, HALF]), func=ACTF.Sin,
                                 scale=-2.0 * math.pi)
            nc.scalar.activation(out=slots[:, tb, 1:3, :], in_=sin_w[:, tb], func=ACTF.Sin, scale=-2.0 * math.pi)

        nc.vector.memset(w_planes[2][:, 1:4, :].bitcast(I32), 0)

        load_scales(w_planes[2], w_scales, NT * 3, NT * 3)
        load_codes(w_codes[3], w_words, 2 * NT * 3, 2 * NT, 0, PASSES)
        load_codes(w_codes[4], w_words, 2 * NT * 4, 2 * NT, 0, PASSES)
        load_codes(w_codes[5], w_words, 2 * NT * 5, 2 * NT, 0, PASSES)

        plane_of = {}
        for i, grp in enumerate(PLANE_GROUPS):
            for j, c in enumerate(grp):
                plane_of[c] = (i, j)

        def passes(acc, c, tb, col0, ncols, g0=0, g1=PASSES):
            i, j = plane_of[c]
            for g in range(g0, g1):
                nc.tensor.matmul_mx(
                    out=acc,
                    lhsT=hs_codes[:, g, 2 * P * tb : 2 * P * (tb + 1)].bitcast(FP4X4),
                    lhsT_scale=hs_planes[:, g, P * tb : P * (tb + 1)],
                    rhs=w_codes[c][:, g, 2 * col0 : 2 * (col0 + ncols)].bitcast(FP4X4),
                    rhs_scale=w_planes[i][:, g, NT * j + col0 : NT * j + col0 + ncols],
                    start=(g == 0),
                    stop=(g == PASSES - 1),
                )

        def products(acc, tb, et):
            nc.vector.tensor_tensor(
                out=et.rearrange("p u (h c) -> p u h c", c=2 * HALF),
                in0=acc.unsqueeze(1).to_broadcast([P, 2, NT]).rearrange("p u (h c) -> p u h c", c=2 * HALF),
                in1=rot[:, tb].rearrange("p u t d -> p u (t d)").unsqueeze(2).to_broadcast([P, 2, 4, 2 * HALF]),
                op=ALU.mult,
            )

        def add_halves(engine, yt, et):
            e5 = et.rearrange("p u j (h t d) -> p (j h) u t d", t=2, d=HALF)
            engine.tensor_tensor(out=yt.rearrange("p j (h u d) -> p (j h) u d", u=2, d=HALF),
                                 in0=e5[:, :, :, 0, :], in1=e5[:, :, :, 1, :], op=ALU.add)

        def values(tb, widths):
            vt = work.tile([P, NT], F32, name="vt", align_bytes=256)
            col0 = 0
            for ncols in widths:
                acc = psum.tile([P, NT], F32, name="acc")
                passes(acc[:, 0:ncols], 5, tb, col0, ncols)
                nc.scalar.copy(out=vt[:, col0 : col0 + ncols], in_=acc[:, 0:ncols])
                col0 += ncols
                nc.scalar.dma_start(out=v2d[P * tb : P * (tb + 1), col0 - ncols : col0], in_=vt[:, col0 - ncols : col0])

        late = []
        first = [psum.tile([P, NT], F32, name="acc") for tb in range(TB)]
        for tb in range(TB):
            passes(first[tb][:], 0, tb, 0, NT, 0, 1)
        for c in range(5):
            for half in range(2):
                et = work.tile([P, 2, 2, NT], F32, name="et", align_bytes=256)
                yt = work.tile([P, 2, NT], F32, name="yt", align_bytes=256)
                for j in range(2):
                    tb = 2 * half + j
                    if c == 0:
                        acc = first[tb]
                        passes(acc[:], c, tb, 0, NT, 1, PASSES)
                    else:
                        acc = psum.tile([P, NT], F32, name="acc")
                        passes(acc[:], c, tb, 0, NT)
                    products(acc[:], tb, et[:, :, j, :])
                    if (c == 4 or c == 0) and half == 0:
                        add_halves(nc.gpsimd, yt[:, j : j + 1, :], et[:, :, j : j + 1, :])
                        nc.sync.dma_start(out=dest(c)[P * tb : P * (tb + 1), :], in_=yt[:, j, :])
                if 0 < c < 3 or (c == 0 and half == 1):
                    add_halves(nc.gpsimd, yt[:], et[:])
                    nc.sync.dma_start(
                        out=dest(c)[2 * P * half : 2 * P * (half + 1), :].rearrange("(t p) n -> p t n", p=P),
                        in_=yt[:],
                    )
                elif c == 3 or half == 1:
                    late.append((half, et, yt))
            if c >= 3:
                for half, et, yt in late:
                    for j in range(2):
                        tb = 2 * half + j
                        add_halves(nc.vector, yt[:, j : j + 1, :], et[:, :, j : j + 1, :])
                        nc.sync.dma_start(out=dest(c)[P * tb : P * (tb + 1), :], in_=yt[:, j, :])
                late = []
            for tb in V_AFTER.get(c, []):
                values(tb, [NT])
        for tb in V_LAST[:-1]:
            values(tb, [NT])
        values(V_LAST[-1], LAST_WIDTHS)
